import numpy as np
import ml_dtypes


def mxq(x, axis, fmt="e4m3"):
    dtype, down = {"e4m3": (ml_dtypes.float8_e4m3fn, 7), "e5m2": (ml_dtypes.float8_e5m2, 14)}[fmt]
    v = np.moveaxis(np.asarray(x, np.float32).astype(ml_dtypes.bfloat16).astype(np.float64), axis, -1)
    blocks = v.reshape(v.shape[:-1] + (-1, 32))
    amax = np.abs(blocks).max(-1, keepdims=True)
    byte = np.maximum(np.where(amax > 0, np.frexp(amax)[1] - 1 + 127, 0) - down, 1)
    scale = np.exp2(byte - 127.0)
    codes = (blocks / scale).astype(np.float32).astype(dtype).astype(np.float64)
    return np.moveaxis((codes * scale).reshape(v.shape), -1, axis)


WIDE = False


def mx_kscale(k):
    if not WIDE:
        return np.ones(k)
    levels = np.array([10, -10, 5, -5, 0])
    a = np.random.permutation(np.resize(levels, k // 512 * 4)).reshape(k // 512, 4)
    idx = np.arange(k)
    return np.exp2(a[idx // 512, idx % 128 // 32])


BF16 = ml_dtypes.bfloat16


def bf(x):
    return np.asarray(x, np.float32).astype(BF16)


def f64(x):
    return np.asarray(x).astype(np.float64)


E2M1 = np.array([0.0, 0.5, 1.0, 1.5, 2.0, 3.0, 4.0, 6.0, -0.0, -0.5, -1.0, -1.5, -2.0, -3.0, -4.0, -6.0])


def pack_weight(w, fmt):
    k, n = w.shape
    w = f64(bf(w)).reshape(k // 32, 32, n)
    amax = np.abs(w).max(1)
    if fmt == "e4m3":
        byte = np.frexp(amax)[1] - 1 + 127 - 7
    else:
        mant, ex = np.frexp(amax / 6.0)
        byte = np.where(mant > 0.5, ex, ex - 1) + 127
    byte = np.clip(np.where(amax > 0, byte, 1), 1, 254)
    scaled = (w * np.exp2(127.0 - byte)[:, None, :]).reshape(k, n).astype(np.float32)
    by_word = np.ascontiguousarray(scaled.reshape(k // 512, 128, 4, n).transpose(0, 1, 3, 2))
    if fmt == "e4m3":
        words = by_word.astype(ml_dtypes.float8_e4m3fn).view(np.uint8)
    else:
        c = by_word.astype(ml_dtypes.float4_e2m1fn).view(np.uint8) & 0xF
        words = c[..., 0::2] | (c[..., 1::2] << 4)
    return np.ascontiguousarray(words), np.ascontiguousarray(byte.astype(np.uint8).reshape(k // 512, 16, n))


def unpack_weight(words, scales, fmt):
    g, p, n, _ = words.shape
    if fmt == "e4m3":
        vals = np.ascontiguousarray(words).view(ml_dtypes.float8_e4m3fn).astype(np.float64)
    else:
        nib = np.empty((g, p, n, 4), np.uint8)
        nib[..., 0::2] = words & 0xF
        nib[..., 1::2] = words >> 4
        vals = E2M1[nib]
    vals = vals * np.repeat(np.exp2(scales.astype(np.float64) - 127.0), 8, axis=1)[..., None]
    return vals.transpose(0, 1, 3, 2).reshape(g * 512, n)


N, C0, H, KS, P, C, O, F, NC = 512, 1, 4, 3, 2, 512, 512, 512, 10
KK = KS * KS
OH = H - KS + 1
OP = OH // P
FC = O * OP * OP


def relu(v):
    return np.maximum(v, 0.0)


def maxpool(v):
    n, c, hh, ww = v.shape
    hp, wp = hh // P, ww // P
    return v[:, :, :hp * P, :wp * P].reshape(n, c, hp, P, wp, P).max(axis=(3, 5))


def setup_inputs():
    s = mx_kscale(C)
    t = mx_kscale(FC)
    tt = np.repeat(np.repeat(t.reshape(O, OP, OP), P, axis=1), P, axis=2)
    h = np.maximum(np.random.standard_normal((P * P, N, C, H, H)).max(0), 0.0)
    w2 = bf(np.random.standard_normal((O, C, KK, OH, OH)) * 0.8 / np.sqrt(KK * C) / s[None, :, None, None, None] * tt[:, None, None, :, :])
    b2 = bf(np.random.standard_normal((O, OH, OH)) * 0.3 * tt)
    fc1_w_words, fc1_w_scales = pack_weight(np.random.standard_normal((FC, F)) * 0.8 / np.sqrt(FC) / t[:, None], "e4m3")
    fc1_b = bf(np.random.standard_normal(F) * 0.3)
    return {
        "h_pool1": bf(h * s[None, :, None, None]),
        "w2": w2,
        "b2": b2,
        "fc1_w_words": fc1_w_words,
        "fc1_w_scales": fc1_w_scales,
        "fc1_b": fc1_b,
    }


def reference(h_pool1, w2, b2, fc1_w_words, fc1_w_scales, fc1_b):
    hq = mxq(f64(h_pool1).transpose(2, 3, 0, 1), 3, "e4m3")
    wq = mxq(f64(w2).transpose(2, 3, 4, 1, 0), 3, "e4m3")
    y = sum((hq[i:i + OH, j:j + OH] @ wq[i * KS + j]) for i in range(KS) for j in range(KS))
    y = y.transpose(2, 3, 0, 1) + f64(b2)
    g = maxpool(relu(y)).reshape(N, FC)
    return relu((mxq(g, 1, "e4m3") @ unpack_weight(fc1_w_words, fc1_w_scales, "e4m3")) + f64(fc1_b))

@@ -1,0 +1,221 @@
+from contextlib import ExitStack
+
+import concourse.mybir as mybir
+from concourse.masks import make_identity
+
+BF16 = mybir.dt.bfloat16
+F32 = mybir.dt.float32
+I32 = mybir.dt.int32
+U32 = mybir.dt.uint32
+U8 = mybir.dt.uint8
+FP8X4 = mybir.dt.float8_e4m3fn_x4
+ADD = mybir.AluOpType.add
+MAX = mybir.AluOpType.max
+RELU = mybir.ActivationFunctionType.Relu
+
+P = 128
+PACK = 4
+BATCH = 512
+CHANNELS = 512
+SIDE = 4
+PIXELS = SIDE * SIDE
+KS = 3
+OFFSETS = KS * KS
+OUT_SIDE = 2
+POSITIONS = OUT_SIDE * OUT_SIDE
+PLANES = OFFSETS * POSITIONS
+OUT_CHANNELS = 512
+FEATURES = 512
+BATCH_TILES = BATCH // P
+O_GROUPS = OUT_CHANNELS // P
+
+FLOPS = 2 * BATCH * CHANNELS * OUT_CHANNELS * PLANES + 2 * BATCH * OUT_CHANNELS * FEATURES
+
+
+def tile_locallyconnectednet_pa_t_kernel(
+    tc, h_pool1, w2, b2, fc1_w_words, fc1_w_scales, fc1_b, out
+):
+    nc = tc.nc
+    with ExitStack() as stack:
+        stack.enter_context(tc.manual_schedule())
+        const = stack.enter_context(tc.tile_pool(name="const", bufs=1))
+        h_raw_pool = stack.enter_context(tc.tile_pool(name="h_raw", bufs=BATCH_TILES))
+        w_raw_pool = stack.enter_context(tc.tile_pool(name="w_raw", bufs=2))
+        grouped_pool = stack.enter_context(tc.tile_pool(name="grouped", bufs=3))
+        w_mx_pool = stack.enter_context(tc.tile_pool(name="w_mx", bufs=4))
+        tail_pool = stack.enter_context(tc.tile_pool(name="tail", bufs=2))
+        bank_pool = stack.enter_context(tc.psum_pool(name="bank", bufs=4))
+        acc_pool = stack.enter_context(tc.psum_pool(name="acc", bufs=1))
+
+        ident = const.tile([P, P], F32)
+        make_identity(nc, ident[:])
+
+        def channels_to_partitions(raw, words_per_channel, pair):
+            words = raw[:].bitcast(F32)
+            bank = bank_pool.tile([P, PACK, P], F32)
+            for t in range(PACK):
+                first = words_per_channel * t + pair
+                nc.tensor.transpose(
+                    bank[:, t, :],
+                    words[:, first : CHANNELS * words_per_channel : PACK * words_per_channel],
+                    ident[:],
+                )
+            return bank
+
+        def part_the_pair(bank_index, grouped, bank):
+            halves = bank[:].bitcast(BF16).rearrange("p t (r e) -> p e r t", e=2)
+            if bank_index % 3 == 2:
+                nc.vector.tensor_copy(out=grouped, in_=halves)
+            else:
+                nc.scalar.copy(out=grouped, in_=halves)
+
+        h_rows = h_pool1.rearrange("(a n) c r s -> a n (c r s)", n=P)
+        w_rows = w2.rearrange("(m g) c k i j -> g m (c k i j)", g=O_GROUPS)
+        W_LOAD_PIECES = 4
+
+        def load_w(group):
+            w_raw = w_raw_pool.tile([P, CHANNELS * PLANES], BF16)
+            piece = CHANNELS * PLANES // W_LOAD_PIECES
+            for q in range(W_LOAD_PIECES):
+                cols = slice(q * piece, (q + 1) * piece)
+                nc.sync.dma_start(out=w_raw[:, cols], in_=w_rows[group][:, cols])
+            return w_raw
+
+        b2_bf = const.tile([P, O_GROUPS * POSITIONS], BF16)
+        nc.sync.dma_start(out=b2_bf[:], in_=b2.rearrange("(m g) i j -> m (g i j)", g=O_GROUPS))
+        b2_f32 = const.tile([P, O_GROUPS * POSITIONS], F32)
+        nc.vector.tensor_copy(out=b2_f32[:], in_=b2_bf[:])
+
+        h_raws = []
+        for a in range(BATCH_TILES):
+            h_raw = h_raw_pool.tile([P, CHANNELS * PIXELS], BF16)
+            nc.sync.dma_start(out=h_raw[:], in_=h_rows[a])
+            h_raws.append(h_raw)
+        w_raws = {0: load_w(0), 1: load_w(1)}
+
+        fc_words = const.tile([P, FEATURES * PACK], U8, align_bytes=64)
+        fc_scales = const.tile([P, FEATURES], U8, align_bytes=64)
+        nc.vector.memset(fc_scales[:].bitcast(I32), 0)
+        nc.sync.dma_start(
+            out=fc_words[:].bitcast(I32),
+            in_=fc1_w_words.rearrange("g p n t -> (g p) (n t)").bitcast(I32),
+        )
+        scale_rows = fc1_w_scales.rearrange("g q n -> (g q) n").bitcast(I32)
+        for quadrant in range(4):
+            nc.sync.dma_start(
+                out=fc_scales[32 * quadrant : 32 * quadrant + 4, :].bitcast(I32),
+                in_=scale_rows[4 * quadrant : 4 * quadrant + 4, :],
+            )
+        fc_bias = const.tile([P, FEATURES], BF16)
+        nc.sync.dma_start(out=fc_bias[:], in_=fc1_b.partition_broadcast(P))
+
+        h_codes = const.tile([P, PIXELS, BATCH], U32, align_bytes=64)
+        h_scales = const.tile([P, PIXELS, BATCH], U8, align_bytes=64)
+        H_PAIRS = PIXELS // 2
+        h_steps = [(a, pair) for a in range(BATCH_TILES) for pair in range(H_PAIRS)]
+        h_grouped = {}
+        for step in range(len(h_steps) + 1):
+            if step < len(h_steps):
+                a, pair = h_steps[step]
+                bank = channels_to_partitions(h_raws[a], H_PAIRS, pair)
+                grouped = grouped_pool.tile([P, 2, P, PACK], BF16, name="h_grouped", align_bytes=64)
+                part_the_pair(step, grouped[:], bank)
+                h_grouped[step] = grouped
+            if step >= 1:
+                a, pair = h_steps[step - 1]
+                images = slice(a * P, (a + 1) * P)
+                for e in range(2):
+                    nc.vector.quantize_mx(
+                        out=h_codes[:, 2 * pair + e, images].bitcast(FP8X4),
+                        scales=h_scales[:, 2 * pair + e, images],
+                        in_=h_grouped[step - 1][:, e].rearrange("p r t -> p (r t)"),
+                    )
+
+        g_grouped = const.tile([P, BATCH, PACK], BF16, align_bytes=64)
+        W_PAIRS = PLANES // 2
+        w_steps = [(group, k) for group in range(O_GROUPS) for k in range(OFFSETS)]
+        w_grouped = {}
+        w_codes = {}
+        w_scales = {}
+        acc = {}
+        for step in range(len(w_steps) + 2):
+            if step < len(w_steps):
+                group, k = w_steps[step]
+                grouped = grouped_pool.tile(
+                    [P, OUT_SIDE, 2, P, PACK], BF16, name="w_grouped", align_bytes=64
+                )
+                for i in range(OUT_SIDE):
+                    bank = channels_to_partitions(w_raws[group], W_PAIRS, OUT_SIDE * k + i)
+                    part_the_pair(OUT_SIDE * step + i, grouped[:, i], bank)
+                w_grouped[step] = grouped
+                if k == OFFSETS - 1 and group + 2 < O_GROUPS:
+                    w_raws[group + 2] = load_w(group + 2)
+            if 1 <= step <= len(w_steps):
+                codes = w_mx_pool.tile([P, POSITIONS, P], U32, name="w_codes", align_bytes=64)
+                scales = w_mx_pool.tile([P, POSITIONS, P], U8, name="w_scales", align_bytes=64)
+                nc.vector.quantize_mx(
+                    out=codes[:].rearrange("p s m -> p (s m)").bitcast(FP8X4),
+                    scales=scales[:].rearrange("p s m -> p (s m)"),
+                    in_=w_grouped[step - 1][:].rearrange("p i j m t -> p (i j m t)"),
+                )
+                w_codes[step - 1] = codes
+                w_scales[step - 1] = scales
+            if step >= 2:
+                group, k = w_steps[step - 2]
+                di, dj = divmod(k, KS)
+                for pos in range(POSITIONS):
+                    i, j = divmod(pos, OUT_SIDE)
+                    pixel = (i + di) * SIDE + (j + dj)
+                    if k == 0:
+                        acc[pos] = acc_pool.tile([P, BATCH], F32, name="acc%d" % pos)
+                    nc.tensor.matmul_mx(
+                        out=acc[pos][:],
+                        lhsT=w_codes[step - 2][:, pos, :].bitcast(FP8X4),
+                        lhsT_scale=w_scales[step - 2][:, pos, :],
+                        rhs=h_codes[:, pixel, :].bitcast(FP8X4),
+                        rhs_scale=h_scales[:, pixel, :],
+                        start=(k == 0),
+                        stop=(k == OFFSETS - 1),
+                    )
+                if k == OFFSETS - 1:
+                    best = tail_pool.tile([P, BATCH], F32, name="best")
+                    for pos in range(POSITIONS):
+                        bias = b2_f32[:, POSITIONS * group + pos : POSITIONS * group + pos + 1]
+                        if pos == 0:
+                            nc.vector.tensor_scalar(
+                                out=best[:], in0=acc[pos][:], scalar1=bias, scalar2=0.0, op0=ADD, op1=MAX
+                            )
+                        else:
+                            last = pos == POSITIONS - 1
+                            nc.vector.scalar_tensor_tensor(
+                                out=g_grouped[:, :, group] if last else best[:],
+                                in0=acc[pos][:],
+                                scalar=bias,
+                                in1=best[:],
+                                op0=ADD,
+                                op1=MAX,
+                            )
+
+        g_codes = const.tile([P, BATCH], U32, align_bytes=64)
+        g_scales = const.tile([P, BATCH], U8, align_bytes=64)
+        nc.vector.quantize_mx(
+            out=g_codes[:].bitcast(FP8X4),
+            scales=g_scales[:],
+            in_=g_grouped[:].rearrange("p n t -> p (n t)"),
+        )
+        for a in range(BATCH_TILES):
+            images = slice(a * P, (a + 1) * P)
+            dense = acc_pool.tile([P, FEATURES], F32, name="acc%d" % a)
+            nc.tensor.matmul_mx(
+                out=dense[:],
+                lhsT=g_codes[:, images].bitcast(FP8X4),
+                lhsT_scale=g_scales[:, images],
+                rhs=fc_words[:].bitcast(FP8X4),
+                rhs_scale=fc_scales[:],
+                start=True,
+                stop=True,
+            )
+            result = tail_pool.tile([P, FEATURES], F32, name="result")
+            nc.vector.tensor_tensor(out=result[:], in0=dense[:], in1=fc_bias[:], op=ADD)
+            nc.scalar.activation(out=result[:], in_=result[:], func=RELU)
+            nc.sync.dma_start(out=out[images, :], in_=result[:])

@@ -28,6 +28,8 @@ OUT_CHANNELS = 512
 FEATURES = 512
 BATCH_TILES = BATCH // P
 O_GROUPS = OUT_CHANNELS // P
+W_GROUPS_BY_TRANSPOSE = 2
+W_LOAD_PIECES = 4
 
 FLOPS = 2 * BATCH * CHANNELS * OUT_CHANNELS * PLANES + 2 * BATCH * OUT_CHANNELS * FEATURES
 
@@ -39,8 +41,7 @@ def tile_locallyconnectednet_pa_t_kernel(
     with ExitStack() as stack:
         stack.enter_context(tc.manual_schedule())
         const = stack.enter_context(tc.tile_pool(name="const", bufs=1))
-        h_raw_pool = stack.enter_context(tc.tile_pool(name="h_raw", bufs=BATCH_TILES))
-        w_raw_pool = stack.enter_context(tc.tile_pool(name="w_raw", bufs=2))
+        raw_pool = stack.enter_context(tc.tile_pool(name="raw", bufs=BATCH_TILES))
         grouped_pool = stack.enter_context(tc.tile_pool(name="grouped", bufs=3))
         w_mx_pool = stack.enter_context(tc.tile_pool(name="w_mx", bufs=4))
         tail_pool = stack.enter_context(tc.tile_pool(name="tail", bufs=2))
@@ -62,36 +63,42 @@ def tile_locallyconnectednet_pa_t_kernel(
                 )
             return bank
 
-        def part_the_pair(bank_index, grouped, bank):
+        def part_the_pair(on_vector, grouped, bank):
             halves = bank[:].bitcast(BF16).rearrange("p t (r e) -> p e r t", e=2)
-            if bank_index % 3 == 2:
+            if on_vector:
                 nc.vector.tensor_copy(out=grouped, in_=halves)
             else:
                 nc.scalar.copy(out=grouped, in_=halves)
-
-        h_rows = h_pool1.rearrange("(a n) c r s -> a n (c r s)", n=P)
-        w_rows = w2.rearrange("(m g) c k i j -> g m (c k i j)", g=O_GROUPS)
-        W_LOAD_PIECES = 4
-
-        def load_w(group):
-            w_raw = w_raw_pool.tile([P, CHANNELS * PLANES], BF16)
-            piece = CHANNELS * PLANES // W_LOAD_PIECES
-            for q in range(W_LOAD_PIECES):
-                cols = slice(q * piece, (q + 1) * piece)
-                nc.sync.dma_start(out=w_raw[:, cols], in_=w_rows[group][:, cols])
-            return w_raw
 
         b2_bf = const.tile([P, O_GROUPS * POSITIONS], BF16)
         nc.sync.dma_start(out=b2_bf[:], in_=b2.rearrange("(m g) i j -> m (g i j)", g=O_GROUPS))
         b2_f32 = const.tile([P, O_GROUPS * POSITIONS], F32)
         nc.vector.tensor_copy(out=b2_f32[:], in_=b2_bf[:])
 
+        h_rows = h_pool1.rearrange("(a n) c r s -> a n (c r s)", n=P)
         h_raws = []
         for a in range(BATCH_TILES):
-            h_raw = h_raw_pool.tile([P, CHANNELS * PIXELS], BF16)
+            h_raw = raw_pool.tile([P, CHANNELS * PIXELS], BF16, tag="raw")
             nc.sync.dma_start(out=h_raw[:], in_=h_rows[a])
             h_raws.append(h_raw)
-        w_raws = {0: load_w(0), 1: load_w(1)}
+
+        w_rows = w2.rearrange("(m g) c k i j -> g m (c k i j)", g=O_GROUPS)
+        w_quads = w2.rearrange("(m g) (p t) k i j -> g p m (t k i j)", g=O_GROUPS, t=PACK)
+        w_raws = []
+        for group in range(O_GROUPS):
+            if group < W_GROUPS_BY_TRANSPOSE:
+                w_raw = raw_pool.tile([P, CHANNELS * PLANES], BF16, tag="raw")
+                piece = CHANNELS * PLANES // W_LOAD_PIECES
+                for q in range(W_LOAD_PIECES):
+                    cols = slice(q * piece, (q + 1) * piece)
+                    nc.sync.dma_start(out=w_raw[:, cols], in_=w_rows[group][:, cols])
+            else:
+                w_raw = raw_pool.tile([P, P, PACK * PLANES], BF16, tag="raw")
+                piece = P // W_LOAD_PIECES
+                for q in range(W_LOAD_PIECES):
+                    rows = slice(q * piece, (q + 1) * piece)
+                    nc.sync.dma_start(out=w_raw[:, rows, :], in_=w_quads[group][:, rows, :])
+            w_raws.append(w_raw)
 
         fc_words = const.tile([P, FEATURES * PACK], U8, align_bytes=64)
         fc_scales = const.tile([P, FEATURES], U8, align_bytes=64)
@@ -118,8 +125,8 @@ def tile_locallyconnectednet_pa_t_kernel(
             if step < len(h_steps):
                 a, pair = h_steps[step]
                 bank = channels_to_partitions(h_raws[a], H_PAIRS, pair)
-                grouped = grouped_pool.tile([P, 2, P, PACK], BF16, name="h_grouped", align_bytes=64)
-                part_the_pair(step, grouped[:], bank)
+                grouped = grouped_pool.tile([P, 2, P, PACK], BF16, tag="grouped", align_bytes=64)
+                part_the_pair(step % 3 == 2, grouped[:], bank)
                 h_grouped[step] = grouped
             if step >= 1:
                 a, pair = h_steps[step - 1]
@@ -141,22 +148,28 @@ def tile_locallyconnectednet_pa_t_kernel(
         for step in range(len(w_steps) + 2):
             if step < len(w_steps):
                 group, k = w_steps[step]
-                grouped = grouped_pool.tile(
-                    [P, OUT_SIDE, 2, P, PACK], BF16, name="w_grouped", align_bytes=64
-                )
-                for i in range(OUT_SIDE):
-                    bank = channels_to_partitions(w_raws[group], W_PAIRS, OUT_SIDE * k + i)
-                    part_the_pair(OUT_SIDE * step + i, grouped[:, i], bank)
+                grouped = grouped_pool.tile([P, POSITIONS, P, PACK], BF16, tag="grouped", align_bytes=64)
+                if group < W_GROUPS_BY_TRANSPOSE:
+                    for i in range(OUT_SIDE):
+                        bank = channels_to_partitions(w_raws[group], W_PAIRS, OUT_SIDE * k + i)
+                        part_the_pair(i == 1, grouped[:, OUT_SIDE * i : OUT_SIDE * (i + 1)], bank)
+                else:
+                    planes = w_raws[group][:].rearrange(
+                        "p m (t k s) -> p k m t s", t=PACK, k=OFFSETS
+                    )[:, k]
+                    spread = grouped[:].rearrange("p s m t -> p m t s")
+                    if step % 2 == 1:
+                        nc.vector.tensor_copy(out=spread, in_=planes)
+                    else:
+                        nc.scalar.copy(out=spread, in_=planes)
                 w_grouped[step] = grouped
-                if k == OFFSETS - 1 and group + 2 < O_GROUPS:
-                    w_raws[group + 2] = load_w(group + 2)
             if 1 <= step <= len(w_steps):
                 codes = w_mx_pool.tile([P, POSITIONS, P], U32, name="w_codes", align_bytes=64)
                 scales = w_mx_pool.tile([P, POSITIONS, P], U8, name="w_scales", align_bytes=64)
                 nc.vector.quantize_mx(
                     out=codes[:].rearrange("p s m -> p (s m)").bitcast(FP8X4),
                     scales=scales[:].rearrange("p s m -> p (s m)"),
-                    in_=w_grouped[step - 1][:].rearrange("p i j m t -> p (i j m t)"),
+                    in_=w_grouped[step - 1][:].rearrange("p s m t -> p (s m t)"),
                 )
                 w_codes[step - 1] = codes
                 w_scales[step - 1] = scales

@@ -28,7 +28,7 @@ OUT_CHANNELS = 512
 FEATURES = 512
 BATCH_TILES = BATCH // P
 O_GROUPS = OUT_CHANNELS // P
-W_GROUPS_BY_TRANSPOSE = 2
+W_GROUPS_BY_TRANSPOSE = 1
 W_LOAD_PIECES = 4
 
 FLOPS = 2 * BATCH * CHANNELS * OUT_CHANNELS * PLANES + 2 * BATCH * OUT_CHANNELS * FEATURES
@@ -42,7 +42,7 @@ def tile_locallyconnectednet_pa_t_kernel(
         stack.enter_context(tc.manual_schedule())
         const = stack.enter_context(tc.tile_pool(name="const", bufs=1))
         raw_pool = stack.enter_context(tc.tile_pool(name="raw", bufs=BATCH_TILES))
-        grouped_pool = stack.enter_context(tc.tile_pool(name="grouped", bufs=3))
+        grouped_pool = stack.enter_context(tc.tile_pool(name="grouped", bufs=4))
         w_mx_pool = stack.enter_context(tc.tile_pool(name="w_mx", bufs=4))
         tail_pool = stack.enter_context(tc.tile_pool(name="tail", bufs=2))
         bank_pool = stack.enter_context(tc.psum_pool(name="bank", bufs=4))
@@ -158,7 +158,7 @@ def tile_locallyconnectednet_pa_t_kernel(
                         "p m (t k s) -> p k m t s", t=PACK, k=OFFSETS
                     )[:, k]
                     spread = grouped[:].rearrange("p s m t -> p m t s")
-                    if step % 2 == 1:
+                    if k % 2 == 1:
                         nc.vector.tensor_copy(out=spread, in_=planes)
                     else:
                         nc.scalar.copy(out=spread, in_=planes)
@@ -191,23 +191,27 @@ def tile_locallyconnectednet_pa_t_kernel(
                         stop=(k == OFFSETS - 1),
                     )
                 if k == OFFSETS - 1:
-                    best = tail_pool.tile([P, BATCH], F32, name="best")
-                    for pos in range(POSITIONS):
-                        bias = b2_f32[:, POSITIONS * group + pos : POSITIONS * group + pos + 1]
-                        if pos == 0:
-                            nc.vector.tensor_scalar(
-                                out=best[:], in0=acc[pos][:], scalar1=bias, scalar2=0.0, op0=ADD, op1=MAX
-                            )
-                        else:
-                            last = pos == POSITIONS - 1
-                            nc.vector.scalar_tensor_tensor(
-                                out=g_grouped[:, :, group] if last else best[:],
-                                in0=acc[pos][:],
-                                scalar=bias,
-                                in1=best[:],
-                                op0=ADD,
-                                op1=MAX,
-                            )
+                    row_best = []
+                    for i in range(OUT_SIDE):
+                        left = OUT_SIDE * i
+                        bias = b2_f32[:, POSITIONS * group + left : POSITIONS * group + left + 2]
+                        relu_left = tail_pool.tile([P, BATCH], F32, name="relu_left")
+                        nc.scalar.activation(
+                            out=relu_left[:], in_=acc[left][:], func=RELU, bias=bias[:, 0:1]
+                        )
+                        best = tail_pool.tile([P, BATCH], F32, name="best")
+                        nc.vector.scalar_tensor_tensor(
+                            out=best[:],
+                            in0=acc[left + 1][:],
+                            scalar=bias[:, 1:2],
+                            in1=relu_left[:],
+                            op0=ADD,
+                            op1=MAX,
+                        )
+                        row_best.append(best)
+                    nc.vector.tensor_tensor(
+                        out=g_grouped[:, :, group], in0=row_best[0][:], in1=row_best[1][:], op=MAX
+                    )
 
         g_codes = const.tile([P, BATCH], U32, align_bytes=64)
         g_scales = const.tile([P, BATCH], U8, align_bytes=64)
@@ -228,7 +232,7 @@ def tile_locallyconnectednet_pa_t_kernel(
                 start=True,
                 stop=True,
             )
-            result = tail_pool.tile([P, FEATURES], F32, name="result")
+            result = tail_pool.tile([P, FEATURES], F32, tag="best")
             nc.vector.tensor_tensor(out=result[:], in0=dense[:], in1=fc_bias[:], op=ADD)
             nc.scalar.activation(out=result[:], in_=result[:], func=RELU)
             nc.sync.dma_start(out=out[images, :], in_=result[:])

@@ -28,7 +28,7 @@ OUT_CHANNELS = 512
 FEATURES = 512
 BATCH_TILES = BATCH // P
 O_GROUPS = OUT_CHANNELS // P
-W_GROUPS_BY_TRANSPOSE = 1
+W_GROUPS_BY_TRANSPOSE = 2
 W_LOAD_PIECES = 4
 
 FLOPS = 2 * BATCH * CHANNELS * OUT_CHANNELS * PLANES + 2 * BATCH * OUT_CHANNELS * FEATURES

@@ -30,6 +30,10 @@ BATCH_TILES = BATCH // P
 O_GROUPS = OUT_CHANNELS // P
 W_GROUPS_BY_TRANSPOSE = 2
 W_LOAD_PIECES = 4
+UNITS = O_GROUPS * OFFSETS
+ROUNDS_OF_A_GROUP = ((0, 1), (2, 3), (4, 5), (6, 7), (8,))
+FIRST_ROUND_WITH_COPIES = 8
+UNITS_MULTIPLIED_A_ROUND = 1
 
 FLOPS = 2 * BATCH * CHANNELS * OUT_CHANNELS * PLANES + 2 * BATCH * OUT_CHANNELS * FEATURES
 
@@ -41,9 +45,10 @@ def tile_locallyconnectednet_pa_t_kernel(
     with ExitStack() as stack:
         stack.enter_context(tc.manual_schedule())
         const = stack.enter_context(tc.tile_pool(name="const", bufs=1))
-        raw_pool = stack.enter_context(tc.tile_pool(name="raw", bufs=BATCH_TILES))
+        raw_pool = stack.enter_context(tc.tile_pool(name="raw", bufs=3))
         grouped_pool = stack.enter_context(tc.tile_pool(name="grouped", bufs=4))
-        w_mx_pool = stack.enter_context(tc.tile_pool(name="w_mx", bufs=4))
+        x_mx_pool = stack.enter_context(tc.tile_pool(name="x_mx", bufs=12))
+        y_mx_pool = stack.enter_context(tc.tile_pool(name="y_mx", bufs=8))
         tail_pool = stack.enter_context(tc.tile_pool(name="tail", bufs=2))
         bank_pool = stack.enter_context(tc.psum_pool(name="bank", bufs=4))
         acc_pool = stack.enter_context(tc.psum_pool(name="acc", bufs=1))
@@ -51,9 +56,8 @@ def tile_locallyconnectednet_pa_t_kernel(
         ident = const.tile([P, P], F32)
         make_identity(nc, ident[:])
 
-        def channels_to_partitions(raw, words_per_channel, pair):
-            words = raw[:].bitcast(F32)
-            bank = bank_pool.tile([P, PACK, P], F32)
+        def channels_to_partitions(words, words_per_channel, pair):
+            bank = bank_pool.tile([P, PACK, P], F32, tag="bank")
             for t in range(PACK):
                 first = words_per_channel * t + pair
                 nc.tensor.transpose(
@@ -76,11 +80,12 @@ def tile_locallyconnectednet_pa_t_kernel(
         nc.vector.tensor_copy(out=b2_f32[:], in_=b2_bf[:])
 
         h_rows = h_pool1.rearrange("(a n) c r s -> a n (c r s)", n=P)
-        h_raws = []
-        for a in range(BATCH_TILES):
-            h_raw = raw_pool.tile([P, CHANNELS * PIXELS], BF16, tag="raw")
-            nc.sync.dma_start(out=h_raw[:], in_=h_rows[a])
-            h_raws.append(h_raw)
+        h_words = []
+        for first in range(0, BATCH_TILES, 2):
+            h_raw = raw_pool.tile([P, 2, CHANNELS * PIXELS], BF16, tag="raw")
+            for a in (first, first + 1):
+                nc.sync.dma_start(out=h_raw[:, a - first, :], in_=h_rows[a])
+                h_words.append(h_raw[:, a - first, :].bitcast(F32))
 
         w_rows = w2.rearrange("(m g) c k i j -> g m (c k i j)", g=O_GROUPS)
         w_quads = w2.rearrange("(m g) (p t) k i j -> g p m (t k i j)", g=O_GROUPS, t=PACK)
@@ -124,7 +129,7 @@ def tile_locallyconnectednet_pa_t_kernel(
         for step in range(len(h_steps) + 1):
             if step < len(h_steps):
                 a, pair = h_steps[step]
-                bank = channels_to_partitions(h_raws[a], H_PAIRS, pair)
+                bank = channels_to_partitions(h_words[a], H_PAIRS, pair)
                 grouped = grouped_pool.tile([P, 2, P, PACK], BF16, tag="grouped", align_bytes=64)
                 part_the_pair(step % 3 == 2, grouped[:], bank)
                 h_grouped[step] = grouped
@@ -140,78 +145,117 @@ def tile_locallyconnectednet_pa_t_kernel(
 
         g_grouped = const.tile([P, BATCH, PACK], BF16, align_bytes=64)
         W_PAIRS = PLANES // 2
-        w_steps = [(group, k) for group in range(O_GROUPS) for k in range(OFFSETS)]
-        w_grouped = {}
-        w_codes = {}
-        w_scales = {}
+        grouped_of = {}
+        codes_of = {}
+        scales_of = {}
         acc = {}
-        for step in range(len(w_steps) + 2):
-            if step < len(w_steps):
-                group, k = w_steps[step]
-                grouped = grouped_pool.tile([P, POSITIONS, P, PACK], BF16, tag="grouped", align_bytes=64)
-                if group < W_GROUPS_BY_TRANSPOSE:
-                    for i in range(OUT_SIDE):
-                        bank = channels_to_partitions(w_raws[group], W_PAIRS, OUT_SIDE * k + i)
-                        part_the_pair(i == 1, grouped[:, OUT_SIDE * i : OUT_SIDE * (i + 1)], bank)
-                else:
-                    planes = w_raws[group][:].rearrange(
-                        "p m (t k s) -> p k m t s", t=PACK, k=OFFSETS
-                    )[:, k]
-                    spread = grouped[:].rearrange("p s m t -> p m t s")
-                    if k % 2 == 1:
-                        nc.vector.tensor_copy(out=spread, in_=planes)
+
+        def fetch_by_transposes(unit, rows_for_vector):
+            group, k = divmod(unit, OFFSETS)
+            grouped = grouped_pool.tile([P, POSITIONS, P, PACK], BF16, tag="grouped", align_bytes=64)
+            for i in range(OUT_SIDE):
+                bank = channels_to_partitions(w_raws[group][:].bitcast(F32), W_PAIRS, OUT_SIDE * k + i)
+                part_the_pair(i in rows_for_vector, grouped[:, OUT_SIDE * i : OUT_SIDE * (i + 1)], bank)
+            grouped_of[unit] = grouped
+
+        def fetch_by_copy(unit, on_vector):
+            group, k = divmod(unit, OFFSETS)
+            grouped = grouped_pool.tile([P, POSITIONS, P, PACK], BF16, tag="grouped", align_bytes=64)
+            planes = w_raws[group][:].rearrange("p m (t k s) -> p k m t s", t=PACK, k=OFFSETS)[:, k]
+            spread = grouped[:].rearrange("p s m t -> p m t s")
+            if on_vector:
+                nc.vector.tensor_copy(out=spread, in_=planes)
+            else:
+                nc.scalar.copy(out=spread, in_=planes)
+            grouped_of[unit] = grouped
+
+        def quantise(unit):
+            pool = x_mx_pool if unit // OFFSETS < W_GROUPS_BY_TRANSPOSE else y_mx_pool
+            codes = pool.tile([P, POSITIONS, P], U32, name="w_codes", align_bytes=64)
+            scales = pool.tile([P, POSITIONS, P], U8, name="w_scales", align_bytes=64)
+            nc.vector.quantize_mx(
+                out=codes[:].rearrange("p s m -> p (s m)").bitcast(FP8X4),
+                scales=scales[:].rearrange("p s m -> p (s m)"),
+                in_=grouped_of[unit][:].rearrange("p s m t -> p (s m t)"),
+            )
+            codes_of[unit] = codes
+            scales_of[unit] = scales
+
+        def multiply(unit):
+            group, k = divmod(unit, OFFSETS)
+            di, dj = divmod(k, KS)
+            for pos in range(POSITIONS):
+                i, j = divmod(pos, OUT_SIDE)
+                pixel = (i + di) * SIDE + (j + dj)
+                if k == 0:
+                    if group % 2 == 1:
+                        acc[pos] = bank_pool.tile([P, BATCH], F32, tag="bank", name="late_acc")
                     else:
-                        nc.scalar.copy(out=spread, in_=planes)
-                w_grouped[step] = grouped
-            if 1 <= step <= len(w_steps):
-                codes = w_mx_pool.tile([P, POSITIONS, P], U32, name="w_codes", align_bytes=64)
-                scales = w_mx_pool.tile([P, POSITIONS, P], U8, name="w_scales", align_bytes=64)
-                nc.vector.quantize_mx(
-                    out=codes[:].rearrange("p s m -> p (s m)").bitcast(FP8X4),
-                    scales=scales[:].rearrange("p s m -> p (s m)"),
-                    in_=w_grouped[step - 1][:].rearrange("p s m t -> p (s m t)"),
-                )
-                w_codes[step - 1] = codes
-                w_scales[step - 1] = scales
-            if step >= 2:
-                group, k = w_steps[step - 2]
-                di, dj = divmod(k, KS)
-                for pos in range(POSITIONS):
-                    i, j = divmod(pos, OUT_SIDE)
-                    pixel = (i + di) * SIDE + (j + dj)
-                    if k == 0:
                         acc[pos] = acc_pool.tile([P, BATCH], F32, name="acc%d" % pos)
-                    nc.tensor.matmul_mx(
-                        out=acc[pos][:],
-                        lhsT=w_codes[step - 2][:, pos, :].bitcast(FP8X4),
-                        lhsT_scale=w_scales[step - 2][:, pos, :],
-                        rhs=h_codes[:, pixel, :].bitcast(FP8X4),
-                        rhs_scale=h_scales[:, pixel, :],
-                        start=(k == 0),
-                        stop=(k == OFFSETS - 1),
+                nc.tensor.matmul_mx(
+                    out=acc[pos][:],
+                    lhsT=codes_of[unit][:, pos, :].bitcast(FP8X4),
+                    lhsT_scale=scales_of[unit][:, pos, :],
+                    rhs=h_codes[:, pixel, :].bitcast(FP8X4),
+                    rhs_scale=h_scales[:, pixel, :],
+                    start=(k == 0),
+                    stop=(k == OFFSETS - 1),
+                )
+            if k == OFFSETS - 1:
+                row_best = []
+                for i in range(OUT_SIDE):
+                    left = OUT_SIDE * i
+                    bias = b2_f32[:, POSITIONS * group + left : POSITIONS * group + left + 2]
+                    relu_left = tail_pool.tile([P, BATCH], F32, name="relu_left")
+                    nc.scalar.activation(
+                        out=relu_left[:], in_=acc[left][:], func=RELU, bias=bias[:, 0:1]
                     )
-                if k == OFFSETS - 1:
-                    row_best = []
-                    for i in range(OUT_SIDE):
-                        left = OUT_SIDE * i
-                        bias = b2_f32[:, POSITIONS * group + left : POSITIONS * group + left + 2]
-                        relu_left = tail_pool.tile([P, BATCH], F32, name="relu_left")
-                        nc.scalar.activation(
-                            out=relu_left[:], in_=acc[left][:], func=RELU, bias=bias[:, 0:1]
-                        )
-                        best = tail_pool.tile([P, BATCH], F32, name="best")
-                        nc.vector.scalar_tensor_tensor(
-                            out=best[:],
-                            in0=acc[left + 1][:],
-                            scalar=bias[:, 1:2],
-                            in1=relu_left[:],
-                            op0=ADD,
-                            op1=MAX,
-                        )
-                        row_best.append(best)
-                    nc.vector.tensor_tensor(
-                        out=g_grouped[:, :, group], in0=row_best[0][:], in1=row_best[1][:], op=MAX
+                    best = tail_pool.tile([P, BATCH], F32, name="best")
+                    nc.vector.scalar_tensor_tensor(
+                        out=best[:],
+                        in0=acc[left + 1][:],
+                        scalar=bias[:, 1:2],
+                        in1=relu_left[:],
+                        op0=ADD,
+                        op1=MAX,
                     )
+                    row_best.append(best)
+                nc.vector.tensor_tensor(
+                    out=g_grouped[:, :, group], in0=row_best[0][:], in1=row_best[1][:], op=MAX
+                )
+
+        rounds = [
+            [OFFSETS * group + k for k in ks]
+            for group in range(W_GROUPS_BY_TRANSPOSE)
+            for ks in ROUNDS_OF_A_GROUP
+        ]
+        copied = list(range(OFFSETS * W_GROUPS_BY_TRANSPOSE, UNITS))
+        to_multiply = list(range(UNITS))
+        ready = []
+        for r, units in enumerate(rounds):
+            early = []
+            if r >= FIRST_ROUND_WITH_COPIES and copied:
+                early.append(copied.pop(0))
+                fetch_by_copy(early[0], True)
+            for unit in units:
+                fetch_by_transposes(unit, () if early else (1,))
+            for unit in early + units:
+                quantise(unit)
+            for n in range(UNITS_MULTIPLIED_A_ROUND):
+                if to_multiply[0] in ready:
+                    multiply(to_multiply.pop(0))
+            ready = ready + early + units
+        fetched = []
+        while to_multiply:
+            for unit in fetched:
+                quantise(unit)
+            for n in range(2):
+                if to_multiply and to_multiply[0] in codes_of:
+                    multiply(to_multiply.pop(0))
+            fetched = [unit for unit in copied[:2] if unit // OFFSETS == copied[0] // OFFSETS]
+            copied = copied[len(fetched) :]
+            for n, unit in enumerate(fetched):
+                fetch_by_copy(unit, n == 1)
 
         g_codes = const.tile([P, BATCH], U32, align_bytes=64)
         g_scales = const.tile([P, BATCH], U8, align_bytes=64)
@@ -222,7 +266,7 @@ def tile_locallyconnectednet_pa_t_kernel(
         )
         for a in range(BATCH_TILES):
             images = slice(a * P, (a + 1) * P)
-            dense = acc_pool.tile([P, FEATURES], F32, name="acc%d" % a)
+            dense = bank_pool.tile([P, FEATURES], F32, tag="bank")
             nc.tensor.matmul_mx(
                 out=dense[:],
                 lhsT=g_codes[:, images].bitcast(FP8X4),
@@ -232,7 +276,7 @@ def tile_locallyconnectednet_pa_t_kernel(
                 start=True,
                 stop=True,
             )
-            result = tail_pool.tile([P, FEATURES], F32, tag="best")
+            result = tail_pool.tile([P, FEATURES], F32, tag=("best", "relu_left")[a % 2], name="result")
             nc.vector.tensor_tensor(out=result[:], in0=dense[:], in1=fc_bias[:], op=ADD)
             nc.scalar.activation(out=result[:], in_=result[:], func=RELU)
             nc.sync.dma_start(out=out[images, :], in_=result[:])

@@ -149,6 +149,7 @@ def tile_locallyconnectednet_pa_t_kernel(
         codes_of = {}
         scales_of = {}
         acc = {}
+        sums_of = {}
 
         def fetch_by_transposes(unit, rows_for_vector):
             group, k = divmod(unit, OFFSETS)
@@ -168,6 +169,20 @@ def tile_locallyconnectednet_pa_t_kernel(
             else:
                 nc.scalar.copy(out=spread, in_=planes)
             grouped_of[unit] = grouped
+
+        def fetch_rows(unit, piece, on_vector):
+            group, k = divmod(unit, OFFSETS)
+            if unit not in grouped_of:
+                grouped_of[unit] = grouped_pool.tile(
+                    [P, POSITIONS, P, PACK], BF16, tag="grouped", align_bytes=64, name="grouped"
+                )
+            rows = slice(piece * (P // W_LOAD_PIECES), (piece + 1) * (P // W_LOAD_PIECES))
+            planes = w_raws[group][:, rows, :].rearrange("p m (t k s) -> p k m t s", t=PACK, k=OFFSETS)[:, k]
+            spread = grouped_of[unit][:, :, rows, :].rearrange("p s m t -> p m t s")
+            if on_vector:
+                nc.vector.tensor_copy(out=spread, in_=planes)
+            else:
+                nc.scalar.copy(out=spread, in_=planes)
 
         def quantise(unit):
             pool = x_mx_pool if unit // OFFSETS < W_GROUPS_BY_TRANSPOSE else y_mx_pool
@@ -202,18 +217,24 @@ def tile_locallyconnectednet_pa_t_kernel(
                     stop=(k == OFFSETS - 1),
                 )
             if k == OFFSETS - 1:
+                sums_of[group] = dict(acc)
+                if group != O_GROUPS - 2:
+                    pooling(group)
+
+        def pooling(group):
+            for sums in (sums_of[group],):
                 row_best = []
                 for i in range(OUT_SIDE):
                     left = OUT_SIDE * i
                     bias = b2_f32[:, POSITIONS * group + left : POSITIONS * group + left + 2]
                     relu_left = tail_pool.tile([P, BATCH], F32, name="relu_left")
                     nc.scalar.activation(
-                        out=relu_left[:], in_=acc[left][:], func=RELU, bias=bias[:, 0:1]
+                        out=relu_left[:], in_=sums[left][:], func=RELU, bias=bias[:, 0:1]
                     )
                     best = tail_pool.tile([P, BATCH], F32, name="best")
                     nc.vector.scalar_tensor_tensor(
                         out=best[:],
-                        in0=acc[left + 1][:],
+                        in0=sums[left + 1][:],
                         scalar=bias[:, 1:2],
                         in1=relu_left[:],
                         op0=ADD,
@@ -246,16 +267,29 @@ def tile_locallyconnectednet_pa_t_kernel(
                     multiply(to_multiply.pop(0))
             ready = ready + early + units
         fetched = []
+        put_off = [O_GROUPS - 2]
         while to_multiply:
             for unit in fetched:
                 quantise(unit)
             for n in range(2):
                 if to_multiply and to_multiply[0] in codes_of:
+                    if UNITS - 1 in codes_of and put_off and O_GROUPS - 2 in sums_of:
+                        pooling(put_off.pop())
                     multiply(to_multiply.pop(0))
-            fetched = [unit for unit in copied[:2] if unit // OFFSETS == copied[0] // OFFSETS]
-            copied = copied[len(fetched) :]
-            for n, unit in enumerate(fetched):
-                fetch_by_copy(unit, n == 1)
+            if copied and copied[0] == OFFSETS * (O_GROUPS - 1):
+                first_units = copied[:2]
+                copied = copied[2:]
+                count = 0
+                for piece in range(W_LOAD_PIECES):
+                    for unit in first_units:
+                        fetch_rows(unit, piece, count % 2 != 0)
+                        count += 1
+                fetched = first_units
+            else:
+                fetched = [unit for unit in copied[:2] if unit // OFFSETS == copied[0] // OFFSETS]
+                copied = copied[len(fetched) :]
+                for n, unit in enumerate(fetched):
+                    fetch_by_copy(unit, n == 1)
 
         g_codes = const.tile([P, BATCH], U32, align_bytes=64)
         g_scales = const.tile([P, BATCH], U8, align_bytes=64)

@@ -33,6 +33,23 @@ W_LOAD_PIECES = 4
 UNITS = O_GROUPS * OFFSETS
 ROUNDS_OF_A_GROUP = ((0, 1), (2, 3), (4, 5), (6, 7), (8,))
 FIRST_ROUND_WITH_COPIES = 8
+LATE = 3
+MX_BUFS = 14
+GROUPED_BUFS = 4
+VEC_BANKS = ((1,), (), (1,))
+MX_IN_ROUND = (0, 1, 1, 0, 1, 1, 0, 1, 1, 1)
+EARLY = ((8, 0, 0, 64, True), (9, 1, 0, 64, True), (9, 2, 0, 64, True))
+SPLIT = 48
+MX_D2 = (1, 1, 2, 1, 1, 2, 1, 1, 2)
+PRE = ((0, 96),)
+MX_PRE = 5
+PRE_V = (3, 5)
+LAST_V = ()
+BEGUN_V = (0, 1, 2)
+EARLY_BUFS = 3
+H_V = ((1,), 3)
+POOL_LAG = (1, 1, 2)
+HALVES = (slice(0, BATCH // 2), slice(BATCH // 2, BATCH))
 UNITS_MULTIPLIED_A_ROUND = 1
 
 FLOPS = 2 * BATCH * CHANNELS * OUT_CHANNELS * PLANES + 2 * BATCH * OUT_CHANNELS * FEATURES
@@ -46,9 +63,9 @@ def tile_locallyconnectednet_pa_t_kernel(
         stack.enter_context(tc.manual_schedule())
         const = stack.enter_context(tc.tile_pool(name="const", bufs=1))
         raw_pool = stack.enter_context(tc.tile_pool(name="raw", bufs=3))
-        grouped_pool = stack.enter_context(tc.tile_pool(name="grouped", bufs=4))
-        x_mx_pool = stack.enter_context(tc.tile_pool(name="x_mx", bufs=12))
-        y_mx_pool = stack.enter_context(tc.tile_pool(name="y_mx", bufs=8))
+        grouped_pool = stack.enter_context(tc.tile_pool(name="grouped", bufs=GROUPED_BUFS))
+        early_pool = stack.enter_context(tc.tile_pool(name="early", bufs=EARLY_BUFS))
+        mx_pool = stack.enter_context(tc.tile_pool(name="mx", bufs=MX_BUFS))
         tail_pool = stack.enter_context(tc.tile_pool(name="tail", bufs=2))
         bank_pool = stack.enter_context(tc.psum_pool(name="bank", bufs=4))
         acc_pool = stack.enter_context(tc.psum_pool(name="acc", bufs=1))
@@ -131,7 +148,7 @@ def tile_locallyconnectednet_pa_t_kernel(
                 a, pair = h_steps[step]
                 bank = channels_to_partitions(h_words[a], H_PAIRS, pair)
                 grouped = grouped_pool.tile([P, 2, P, PACK], BF16, tag="grouped", align_bytes=64)
-                part_the_pair(step % 3 == 2, grouped[:], bank)
+                part_the_pair(step % H_V[1] in H_V[0], grouped[:], bank)
                 h_grouped[step] = grouped
             if step >= 1:
                 a, pair = h_steps[step - 1]
@@ -144,6 +161,7 @@ def tile_locallyconnectednet_pa_t_kernel(
                     )
 
         g_grouped = const.tile([P, BATCH, PACK], BF16, align_bytes=64)
+        g_lines = const.tile([P, PACK, BATCH], BF16, align_bytes=64)
         W_PAIRS = PLANES // 2
         grouped_of = {}
         codes_of = {}
@@ -151,32 +169,23 @@ def tile_locallyconnectednet_pa_t_kernel(
         acc = {}
         sums_of = {}
 
-        def fetch_by_transposes(unit, rows_for_vector):
+        def fetch_by_transposes(unit, for_vector):
             group, k = divmod(unit, OFFSETS)
             grouped = grouped_pool.tile([P, POSITIONS, P, PACK], BF16, tag="grouped", align_bytes=64)
             for i in range(OUT_SIDE):
                 bank = channels_to_partitions(w_raws[group][:].bitcast(F32), W_PAIRS, OUT_SIDE * k + i)
-                part_the_pair(i in rows_for_vector, grouped[:, OUT_SIDE * i : OUT_SIDE * (i + 1)], bank)
-            grouped_of[unit] = grouped
+                part_the_pair(i in for_vector, grouped[:, OUT_SIDE * i : OUT_SIDE * (i + 1)], bank)
+            grouped_of[unit] = grouped[:]
 
-        def fetch_by_copy(unit, on_vector):
-            group, k = divmod(unit, OFFSETS)
-            grouped = grouped_pool.tile([P, POSITIONS, P, PACK], BF16, tag="grouped", align_bytes=64)
-            planes = w_raws[group][:].rearrange("p m (t k s) -> p k m t s", t=PACK, k=OFFSETS)[:, k]
-            spread = grouped[:].rearrange("p s m t -> p m t s")
-            if on_vector:
-                nc.vector.tensor_copy(out=spread, in_=planes)
-            else:
-                nc.scalar.copy(out=spread, in_=planes)
-            grouped_of[unit] = grouped
-
-        def fetch_rows(unit, piece, on_vector):
+        def copy_rows(unit, first, last, on_vector):
             group, k = divmod(unit, OFFSETS)
             if unit not in grouped_of:
-                grouped_of[unit] = grouped_pool.tile(
+                early = unit - OFFSETS * 2 in {e[1] for e in EARLY}
+                tile = (early_pool if early else grouped_pool).tile(
                     [P, POSITIONS, P, PACK], BF16, tag="grouped", align_bytes=64, name="grouped"
                 )
-            rows = slice(piece * (P // W_LOAD_PIECES), (piece + 1) * (P // W_LOAD_PIECES))
+                grouped_of[unit] = tile[:]
+            rows = slice(first, last)
             planes = w_raws[group][:, rows, :].rearrange("p m (t k s) -> p k m t s", t=PACK, k=OFFSETS)[:, k]
             spread = grouped_of[unit][:, :, rows, :].rearrange("p s m t -> p m t s")
             if on_vector:
@@ -185,122 +194,163 @@ def tile_locallyconnectednet_pa_t_kernel(
                 nc.scalar.copy(out=spread, in_=planes)
 
         def quantise(unit):
-            pool = x_mx_pool if unit // OFFSETS < W_GROUPS_BY_TRANSPOSE else y_mx_pool
-            codes = pool.tile([P, POSITIONS, P], U32, name="w_codes", align_bytes=64)
-            scales = pool.tile([P, POSITIONS, P], U8, name="w_scales", align_bytes=64)
+            codes = mx_pool.tile([P, POSITIONS, P], U32, name="w_codes", align_bytes=64)
+            scales = mx_pool.tile([P, POSITIONS, P], U8, name="w_scales", align_bytes=64)
             nc.vector.quantize_mx(
                 out=codes[:].rearrange("p s m -> p (s m)").bitcast(FP8X4),
                 scales=scales[:].rearrange("p s m -> p (s m)"),
-                in_=grouped_of[unit][:].rearrange("p s m t -> p (s m t)"),
+                in_=grouped_of[unit].rearrange("p s m t -> p (s m t)"),
             )
             codes_of[unit] = codes
             scales_of[unit] = scales
 
-        def multiply(unit):
+        def pass_of(unit, pos):
             group, k = divmod(unit, OFFSETS)
             di, dj = divmod(k, KS)
-            for pos in range(POSITIONS):
-                i, j = divmod(pos, OUT_SIDE)
-                pixel = (i + di) * SIDE + (j + dj)
-                if k == 0:
-                    if group % 2 == 1:
-                        acc[pos] = bank_pool.tile([P, BATCH], F32, tag="bank", name="late_acc")
-                    else:
-                        acc[pos] = acc_pool.tile([P, BATCH], F32, name="acc%d" % pos)
-                nc.tensor.matmul_mx(
-                    out=acc[pos][:],
-                    lhsT=codes_of[unit][:, pos, :].bitcast(FP8X4),
-                    lhsT_scale=scales_of[unit][:, pos, :],
-                    rhs=h_codes[:, pixel, :].bitcast(FP8X4),
-                    rhs_scale=h_scales[:, pixel, :],
-                    start=(k == 0),
-                    stop=(k == OFFSETS - 1),
-                )
+            i, j = divmod(pos, OUT_SIDE)
+            pixel = (i + di) * SIDE + (j + dj)
+            if k == 0:
+                if group % 2 == 1:
+                    acc[pos] = bank_pool.tile([P, BATCH], F32, tag="bank", name="late_acc")
+                else:
+                    acc[pos] = acc_pool.tile([P, BATCH], F32, name="acc%d" % pos)
+            nc.tensor.matmul_mx(
+                out=acc[pos][:],
+                lhsT=codes_of[unit][:, pos, :].bitcast(FP8X4),
+                lhsT_scale=scales_of[unit][:, pos, :],
+                rhs=h_codes[:, pixel, :].bitcast(FP8X4),
+                rhs_scale=h_scales[:, pixel, :],
+                start=(k == 0),
+                stop=(k == OFFSETS - 1),
+            )
+
+        def multiply(unit):
+            group, k = divmod(unit, OFFSETS)
+            if unit >= UNITS - LATE:
+                if unit == UNITS - 1:
+                    for pos in range(POSITIONS):
+                        for late in range(UNITS - LATE, UNITS):
+                            pass_of(late, pos)
+            else:
+                for pos in range(POSITIONS):
+                    pass_of(unit, pos)
             if k == OFFSETS - 1:
                 sums_of[group] = dict(acc)
-                if group != O_GROUPS - 2:
-                    pooling(group)
+                if group < O_GROUPS - 1:
+                    due.append((unit + POOL_LAG[group], group))
+
+        def pool_first(group, images):
+            best = tail_pool.tile([P, images.stop - images.start], F32, tag="best", name="best")
+            nc.scalar.activation(
+                out=best[:],
+                in_=sums_of[group][0][:, images],
+                func=RELU,
+                bias=b2_f32[:, POSITIONS * group : POSITIONS * group + 1],
+            )
+            return best
+
+        def pool_next(group, pos, images, best, out):
+            col = POSITIONS * group + pos
+            nc.vector.scalar_tensor_tensor(
+                out=out,
+                in0=sums_of[group][pos][:, images],
+                scalar=b2_f32[:, col : col + 1],
+                in1=best[:],
+                op0=ADD,
+                op1=MAX,
+            )
+
+        def pool_but_the_last(group):
+            images = slice(0, BATCH)
+            best = pool_first(group, images)
+            for pos in (1, 2):
+                better = tail_pool.tile([P, BATCH], F32, tag=("best", "relu_left")[pos % 2], name="better")
+                pool_next(group, pos, images, best, better[:])
+                best = better
+            return best
 
         def pooling(group):
-            for sums in (sums_of[group],):
-                row_best = []
-                for i in range(OUT_SIDE):
-                    left = OUT_SIDE * i
-                    bias = b2_f32[:, POSITIONS * group + left : POSITIONS * group + left + 2]
-                    relu_left = tail_pool.tile([P, BATCH], F32, name="relu_left")
-                    nc.scalar.activation(
-                        out=relu_left[:], in_=sums[left][:], func=RELU, bias=bias[:, 0:1]
-                    )
-                    best = tail_pool.tile([P, BATCH], F32, name="best")
-                    nc.vector.scalar_tensor_tensor(
-                        out=best[:],
-                        in0=sums[left + 1][:],
-                        scalar=bias[:, 1:2],
-                        in1=relu_left[:],
-                        op0=ADD,
-                        op1=MAX,
-                    )
-                    row_best.append(best)
-                nc.vector.tensor_tensor(
-                    out=g_grouped[:, :, group], in0=row_best[0][:], in1=row_best[1][:], op=MAX
-                )
+            best = pool_but_the_last(group)
+            pool_next(group, POSITIONS - 1, slice(0, BATCH), best, g_lines[:, group, :])
+
+        due = []
+        to_multiply = list(range(UNITS))
+        ready = set()
+
+        def multiply_next():
+            if to_multiply and to_multiply[0] in codes_of:
+                unit = to_multiply.pop(0)
+                multiply(unit)
+                while due and due[0][0] <= unit:
+                    pooling(due.pop(0)[1])
 
         rounds = [
             [OFFSETS * group + k for k in ks]
             for group in range(W_GROUPS_BY_TRANSPOSE)
             for ks in ROUNDS_OF_A_GROUP
         ]
-        copied = list(range(OFFSETS * W_GROUPS_BY_TRANSPOSE, UNITS))
-        to_multiply = list(range(UNITS))
-        ready = []
+        third = list(range(OFFSETS * 2, OFFSETS * 3))
+        fourth = list(range(OFFSETS * 3, UNITS))
         for r, units in enumerate(rounds):
-            early = []
-            if r >= FIRST_ROUND_WITH_COPIES and copied:
-                early.append(copied.pop(0))
-                fetch_by_copy(early[0], True)
+            for n, unit in enumerate(units):
+                fetch_by_transposes(unit, VEC_BANKS[r % 2] if n == 0 else VEC_BANKS[2])
+            for rr, n, first, last, vec in EARLY:
+                if rr == r:
+                    copy_rows(third[n], first, last, vec)
             for unit in units:
-                fetch_by_transposes(unit, () if early else (1,))
-            for unit in early + units:
                 quantise(unit)
-            for n in range(UNITS_MULTIPLIED_A_ROUND):
+            for n in range(MX_IN_ROUND[r]):
                 if to_multiply[0] in ready:
-                    multiply(to_multiply.pop(0))
-            ready = ready + early + units
-        fetched = []
-        put_off = [O_GROUPS - 2]
+                    multiply_next()
+            ready.update(units)
+        begun = sorted({e[1] for e in EARLY})
+        for n in begun:
+            copy_rows(third[n], max(e[3] for e in EARLY if e[1] == n), P, n in BEGUN_V)
+        for n, unit in enumerate(third):
+            if n + len(begun) < OFFSETS:
+                copy_rows(third[n + len(begun)], 0, SPLIT, True)
+                copy_rows(third[n + len(begun)], SPLIT, P, False)
+            quantise(unit)
+            for n in range(MX_D2[n]):
+                multiply_next()
+        last_group = raw_pool.tile([P, OFFSETS, POSITIONS, P, PACK], BF16, tag="raw")
+        for n, unit in enumerate(fourth):
+            grouped_of[unit] = last_group[:, n]
+        count = 0
+        for first, last in PRE:
+            for n, unit in enumerate(fourth):
+                copy_rows(unit, first, last, n % PRE_V[1] < PRE_V[0])
+                count += 1
+                if count % MX_PRE == 0:
+                    multiply_next()
+        for n, unit in enumerate(fourth):
+            copy_rows(unit, PRE[-1][1], P, n in LAST_V)
+            if n >= 1:
+                quantise(fourth[n - 1])
+                multiply_next()
+        quantise(fourth[-1])
         while to_multiply:
-            for unit in fetched:
-                quantise(unit)
-            for n in range(2):
-                if to_multiply and to_multiply[0] in codes_of:
-                    if UNITS - 1 in codes_of and put_off and O_GROUPS - 2 in sums_of:
-                        pooling(put_off.pop())
-                    multiply(to_multiply.pop(0))
-            if copied and copied[0] == OFFSETS * (O_GROUPS - 1):
-                first_units = copied[:2]
-                copied = copied[2:]
-                count = 0
-                for piece in range(W_LOAD_PIECES):
-                    for unit in first_units:
-                        fetch_rows(unit, piece, count % 2 != 0)
-                        count += 1
-                fetched = first_units
-            else:
-                fetched = [unit for unit in copied[:2] if unit // OFFSETS == copied[0] // OFFSETS]
-                copied = copied[len(fetched) :]
-                for n, unit in enumerate(fetched):
-                    fetch_by_copy(unit, n == 1)
-
+            multiply_next()
+        best = pool_but_the_last(O_GROUPS - 1)
         g_codes = const.tile([P, BATCH], U32, align_bytes=64)
         g_scales = const.tile([P, BATCH], U8, align_bytes=64)
-        nc.vector.quantize_mx(
-            out=g_codes[:].bitcast(FP8X4),
-            scales=g_scales[:],
-            in_=g_grouped[:].rearrange("p n t -> p (n t)"),
-        )
-        for a in range(BATCH_TILES):
+        for images in HALVES:
+            pool_next(O_GROUPS - 1, POSITIONS - 1, images, best[:, images], g_lines[:, O_GROUPS - 1, images])
+        for n, images in enumerate(HALVES):
+            four = g_lines[:, :, images].rearrange("p t n -> p n t")
+            if n == 0:
+                nc.scalar.copy(out=g_grouped[:, images, :], in_=four)
+            else:
+                nc.vector.tensor_copy(out=g_grouped[:, images, :], in_=four)
+        for images in HALVES[::-1]:
+            nc.vector.quantize_mx(
+                out=g_codes[:, images].bitcast(FP8X4),
+                scales=g_scales[:, images],
+                in_=g_grouped[:, images, :].rearrange("p n t -> p (n t)"),
+            )
+        for n, a in enumerate((2, 3, 0, 1)):
             images = slice(a * P, (a + 1) * P)
-            dense = bank_pool.tile([P, FEATURES], F32, tag="bank")
+            dense = acc_pool.tile([P, FEATURES], F32, name="acc%d" % a)
             nc.tensor.matmul_mx(
                 out=dense[:],
                 lhsT=g_codes[:, images].bitcast(FP8X4),
@@ -310,7 +360,8 @@ def tile_locallyconnectednet_pa_t_kernel(
                 start=True,
                 stop=True,
             )
-            result = tail_pool.tile([P, FEATURES], F32, tag=("best", "relu_left")[a % 2], name="result")
-            nc.vector.tensor_tensor(out=result[:], in0=dense[:], in1=fc_bias[:], op=ADD)
-            nc.scalar.activation(out=result[:], in_=result[:], func=RELU)
+            result = tail_pool.tile([P, FEATURES], F32, tag=("best", "relu_left")[n % 2], name="result")
+            for cols in HALVES if n == 3 else (slice(0, FEATURES),):
+                nc.vector.tensor_tensor(out=result[:, cols], in0=dense[:, cols], in1=fc_bias[:, cols], op=ADD)
+                nc.scalar.activation(out=result[:, cols], in_=result[:, cols], func=RELU)
             nc.sync.dma_start(out=out[images, :], in_=result[:])

@@ -34,21 +34,26 @@ UNITS = O_GROUPS * OFFSETS
 ROUNDS_OF_A_GROUP = ((0, 1), (2, 3), (4, 5), (6, 7), (8,))
 FIRST_ROUND_WITH_COPIES = 8
 LATE = 3
-MX_BUFS = 14
+MX_BUFS = 12
 GROUPED_BUFS = 4
-VEC_BANKS = ((1,), (), (1,))
-MX_IN_ROUND = (0, 1, 1, 0, 1, 1, 0, 1, 1, 1)
+VEC_BANKS = ((), (), ())
+MX_IN_ROUND = (0, 1, 1, 1, 1, 1, 1, 1, 1, 0)
 EARLY = ((8, 0, 0, 64, True), (9, 1, 0, 64, True), (9, 2, 0, 64, True))
-SPLIT = 48
-MX_D2 = (1, 1, 2, 1, 1, 2, 1, 1, 2)
-PRE = ((0, 96),)
-MX_PRE = 5
-PRE_V = (3, 5)
-LAST_V = ()
+SPLIT = 32
+MX_D2 = (1, 1, 1, 2, 1, 1, 1, 2, 1)
+PRE = ((0, 64), (64, 96))
+MX_PRE = 3
+PRE_V = (1, 2)
+LAST_V = (0, 4)
 BEGUN_V = (0, 1, 2)
+STAGE_BUFS = 2
+REORDER = ("V", "")
+FIRST_RE = 1
+VEC_RE = (1,)
+QLATE = True
 EARLY_BUFS = 3
-H_V = ((1,), 3)
-POOL_LAG = (1, 1, 2)
+H_V = ((1, 4, 7), 8)
+POOL_LAG = (2, 1, 3)
 HALVES = (slice(0, BATCH // 2), slice(BATCH // 2, BATCH))
 UNITS_MULTIPLIED_A_ROUND = 1
 
@@ -64,6 +69,7 @@ def tile_locallyconnectednet_pa_t_kernel(
         const = stack.enter_context(tc.tile_pool(name="const", bufs=1))
         raw_pool = stack.enter_context(tc.tile_pool(name="raw", bufs=3))
         grouped_pool = stack.enter_context(tc.tile_pool(name="grouped", bufs=GROUPED_BUFS))
+        stage_pool = stack.enter_context(tc.tile_pool(name="stage", bufs=STAGE_BUFS))
         early_pool = stack.enter_context(tc.tile_pool(name="early", bufs=EARLY_BUFS))
         mx_pool = stack.enter_context(tc.tile_pool(name="mx", bufs=MX_BUFS))
         tail_pool = stack.enter_context(tc.tile_pool(name="tail", bufs=2))
@@ -175,6 +181,37 @@ def tile_locallyconnectednet_pa_t_kernel(
             for i in range(OUT_SIDE):
                 bank = channels_to_partitions(w_raws[group][:].bitcast(F32), W_PAIRS, OUT_SIDE * k + i)
                 part_the_pair(i in for_vector, grouped[:, OUT_SIDE * i : OUT_SIDE * (i + 1)], bank)
+            grouped_of[unit] = grouped[:]
+
+        stage_of = {}
+
+        def reorder(unit, on_vector):
+            group, k = divmod(unit, OFFSETS)
+            stage = stage_pool.tile([P, POSITIONS, 2, P, 2], BF16, tag="stage", align_bytes=64, name="stage")
+            planes = w_raws[group][:].rearrange("m (p u e k s) -> m k u p e s", p=P, u=2, e=2, k=OFFSETS)[:, k]
+            spread = stage[:].rearrange("m s u p e -> m u p e s")
+            if on_vector:
+                nc.vector.tensor_copy(out=spread, in_=planes)
+            else:
+                nc.scalar.copy(out=spread, in_=planes)
+            stage_of[unit] = stage
+
+        def fetch_reordered(unit, for_vector):
+            grouped = grouped_pool.tile([P, POSITIONS, P, PACK], BF16, tag="grouped", align_bytes=64)
+            words = stage_of[unit][:].rearrange("m s u p e -> m (s u p e)").bitcast(F32)
+            for i in range(OUT_SIDE):
+                bank = bank_pool.tile([P, 2, 2, P], F32, tag="bank", name="bank")
+                for s in range(2):
+                    for u in range(2):
+                        first = ((OUT_SIDE * i + s) * 2 + u) * P
+                        nc.tensor.transpose(bank[:, s, u, :], words[:, first : first + P], ident[:])
+                half = grouped[:, OUT_SIDE * i : OUT_SIDE * (i + 1)].rearrange("p s m t -> p (s m t)").bitcast(F32)
+                out = half.rearrange("p (j m u) -> p j m u", j=2, u=2)
+                in_ = bank[:].rearrange("p j u m -> p j m u")
+                if i in for_vector:
+                    nc.vector.tensor_copy(out=out, in_=in_)
+                else:
+                    nc.scalar.copy(out=out, in_=in_)
             grouped_of[unit] = grouped[:]
 
         def copy_rows(unit, first, last, on_vector):
@@ -291,18 +328,37 @@ def tile_locallyconnectednet_pa_t_kernel(
         ]
         third = list(range(OFFSETS * 2, OFFSETS * 3))
         fourth = list(range(OFFSETS * 3, UNITS))
+        for n, unit in enumerate(rounds[0]):
+            if REORDER[n] and FIRST_RE == 0:
+                reorder(unit, REORDER[n] == "V")
+        waiting = []
         for r, units in enumerate(rounds):
-            for n, unit in enumerate(units):
-                fetch_by_transposes(unit, VEC_BANKS[r % 2] if n == 0 else VEC_BANKS[2])
+            if r + 1 < len(rounds):
+                for n, unit in enumerate(rounds[r + 1]):
+                    if REORDER[n] and r + 1 >= FIRST_RE:
+                        reorder(unit, REORDER[n] == "V")
+            if QLATE:
+                for unit in waiting:
+                    quantise(unit)
             for rr, n, first, last, vec in EARLY:
                 if rr == r:
                     copy_rows(third[n], first, last, vec)
-            for unit in units:
-                quantise(unit)
+            for n, unit in enumerate(units):
+                if unit in stage_of:
+                    fetch_reordered(unit, VEC_RE)
+                else:
+                    fetch_by_transposes(unit, VEC_BANKS[r % 2] if n == 0 else VEC_BANKS[2])
+            if not QLATE:
+                for unit in units:
+                    quantise(unit)
             for n in range(MX_IN_ROUND[r]):
                 if to_multiply[0] in ready:
                     multiply_next()
-            ready.update(units)
+            ready.update(units if not QLATE else waiting)
+            waiting = units
+        if QLATE:
+            for unit in waiting:
+                quantise(unit)
         begun = sorted({e[1] for e in EARLY})
         for n in begun:
             copy_rows(third[n], max(e[3] for e in EARLY if e[1] == n), P, n in BEGUN_V)

@@ -98,9 +98,7 @@ def tile_locallyconnectednet_pa_t_kernel(
                 nc.scalar.copy(out=grouped, in_=halves)
 
         b2_bf = const.tile([P, O_GROUPS * POSITIONS], BF16)
-        nc.sync.dma_start(out=b2_bf[:], in_=b2.rearrange("(m g) i j -> m (g i j)", g=O_GROUPS))
         b2_f32 = const.tile([P, O_GROUPS * POSITIONS], F32)
-        nc.vector.tensor_copy(out=b2_f32[:], in_=b2_bf[:])
 
         h_rows = h_pool1.rearrange("(a n) c r s -> a n (c r s)", n=P)
         h_words = []
@@ -109,6 +107,8 @@ def tile_locallyconnectednet_pa_t_kernel(
             for a in (first, first + 1):
                 nc.sync.dma_start(out=h_raw[:, a - first, :], in_=h_rows[a])
                 h_words.append(h_raw[:, a - first, :].bitcast(F32))
+
+        nc.sync.dma_start(out=b2_bf[:], in_=b2.rearrange("(m g) i j -> m (g i j)", g=O_GROUPS))
 
         w_rows = w2.rearrange("(m g) c k i j -> g m (c k i j)", g=O_GROUPS)
         w_quads = w2.rearrange("(m g) (p t) k i j -> g p m (t k i j)", g=O_GROUPS, t=PACK)
@@ -168,6 +168,7 @@ def tile_locallyconnectednet_pa_t_kernel(
 
         g_grouped = const.tile([P, BATCH, PACK], BF16, align_bytes=64)
         g_lines = const.tile([P, PACK, BATCH], BF16, align_bytes=64)
+        nc.vector.tensor_copy(out=b2_f32[:], in_=b2_bf[:])
         W_PAIRS = PLANES // 2
         grouped_of = {}
         codes_of = {}
@@ -306,9 +307,27 @@ def tile_locallyconnectednet_pa_t_kernel(
                 best = better
             return best
 
+        pool_steps = []
+
         def pooling(group):
-            best = pool_but_the_last(group)
-            pool_next(group, POSITIONS - 1, slice(0, BATCH), best, g_lines[:, group, :])
+            images = slice(0, BATCH)
+            best = [pool_first(group, images)]
+
+            def step(pos):
+                if pos < POSITIONS - 1:
+                    better = tail_pool.tile([P, BATCH], F32, tag=("best", "relu_left")[pos % 2], name="better")
+                    pool_next(group, pos, images, best[0], better[:])
+                    best[0] = better
+                else:
+                    pool_next(group, pos, images, best[0], g_lines[:, group, :])
+
+            for pos in range(1, POSITIONS):
+                pool_steps.append((step, pos))
+
+        def pool_step():
+            if pool_steps:
+                step, pos = pool_steps.pop(0)
+                step(pos)
 
         due = []
         to_multiply = list(range(UNITS))
@@ -364,9 +383,11 @@ def tile_locallyconnectednet_pa_t_kernel(
             copy_rows(third[n], max(e[3] for e in EARLY if e[1] == n), P, n in BEGUN_V)
         for n, unit in enumerate(third):
             if n + len(begun) < OFFSETS:
-                copy_rows(third[n + len(begun)], 0, SPLIT, True)
+                if SPLIT > 0:
+                    copy_rows(third[n + len(begun)], 0, SPLIT, True)
                 copy_rows(third[n + len(begun)], SPLIT, P, False)
             quantise(unit)
+            pool_step()
             for n in range(MX_D2[n]):
                 multiply_next()
         last_group = raw_pool.tile([P, OFFSETS, POSITIONS, P, PACK], BF16, tag="raw")
@@ -376,17 +397,26 @@ def tile_locallyconnectednet_pa_t_kernel(
         for first, last in PRE:
             for n, unit in enumerate(fourth):
                 copy_rows(unit, first, last, n % PRE_V[1] < PRE_V[0])
+                if n % PRE_V[1] < PRE_V[0]:
+                    pool_step()
                 count += 1
                 if count % MX_PRE == 0:
                     multiply_next()
         for n, unit in enumerate(fourth):
+            if n == 0:
+                while pool_steps:
+                    pool_step()
             copy_rows(unit, PRE[-1][1], P, n in LAST_V)
             if n >= 1:
                 quantise(fourth[n - 1])
+                pool_step()
                 multiply_next()
         quantise(fourth[-1])
         while to_multiply:
             multiply_next()
+            pool_step()
+        while pool_steps:
+            pool_step()
         best = pool_but_the_last(O_GROUPS - 1)
         g_codes = const.tile([P, BATCH], U32, align_bytes=64)
         g_scales = const.tile([P, BATCH], U8, align_bytes=64)
@@ -420,4 +450,4 @@ def tile_locallyconnectednet_pa_t_kernel(
             for cols in HALVES if n == 3 else (slice(0, FEATURES),):
                 nc.vector.tensor_tensor(out=result[:, cols], in0=dense[:, cols], in1=fc_bias[:, cols], op=ADD)
                 nc.scalar.activation(out=result[:, cols], in_=result[:, cols], func=RELU)
-            nc.sync.dma_start(out=out[images, :], in_=result[:])
+                nc.sync.dma_start(out=out[images, cols], in_=result[:, cols])

from contextlib import ExitStack

import concourse.mybir as mybir
from concourse.masks import make_identity

BF16 = mybir.dt.bfloat16
F32 = mybir.dt.float32
I32 = mybir.dt.int32
U32 = mybir.dt.uint32
U8 = mybir.dt.uint8
FP8X4 = mybir.dt.float8_e4m3fn_x4
ADD = mybir.AluOpType.add
MAX = mybir.AluOpType.max
RELU = mybir.ActivationFunctionType.Relu

P = 128
PACK = 4
BATCH = 512
CHANNELS = 512
SIDE = 4
PIXELS = SIDE * SIDE
KS = 3
OFFSETS = KS * KS
OUT_SIDE = 2
POSITIONS = OUT_SIDE * OUT_SIDE
PLANES = OFFSETS * POSITIONS
OUT_CHANNELS = 512
FEATURES = 512
BATCH_TILES = BATCH // P
O_GROUPS = OUT_CHANNELS // P
W_GROUPS_BY_TRANSPOSE = 2
W_LOAD_PIECES = 4
UNITS = O_GROUPS * OFFSETS
ROUNDS_OF_A_GROUP = ((0, 1), (2, 3), (4, 5), (6, 7), (8,))
FIRST_ROUND_WITH_COPIES = 8
LATE = 3
MX_BUFS = 12
GROUPED_BUFS = 4
VEC_BANKS = ((), (), ())
MX_IN_ROUND = (0, 1, 1, 1, 1, 1, 1, 1, 1, 0)
EARLY = ((8, 0, 0, 64, True), (9, 1, 0, 64, True), (9, 2, 0, 64, True))
SPLIT = 32
MX_D2 = (1, 1, 1, 2, 1, 1, 1, 2, 1)
PRE = ((0, 64), (64, 96))
MX_PRE = 3
PRE_V = (1, 2)
LAST_V = (0, 4)
BEGUN_V = (0, 1, 2)
STAGE_BUFS = 2
REORDER = ("V", "")
FIRST_RE = 1
VEC_RE = (1,)
QLATE = True
EARLY_BUFS = 3
H_V = ((1, 4, 7), 8)
POOL_LAG = (2, 1, 3)
HALVES = (slice(0, BATCH // 2), slice(BATCH // 2, BATCH))
UNITS_MULTIPLIED_A_ROUND = 1

FLOPS = 2 * BATCH * CHANNELS * OUT_CHANNELS * PLANES + 2 * BATCH * OUT_CHANNELS * FEATURES


def tile_locallyconnectednet_pa_t_kernel(
    tc, h_pool1, w2, b2, fc1_w_words, fc1_w_scales, fc1_b, out
):
    nc = tc.nc
    with ExitStack() as stack:
        stack.enter_context(tc.manual_schedule())
        const = stack.enter_context(tc.tile_pool(name="const", bufs=1))
        raw_pool = stack.enter_context(tc.tile_pool(name="raw", bufs=3))
        grouped_pool = stack.enter_context(tc.tile_pool(name="grouped", bufs=GROUPED_BUFS))
        stage_pool = stack.enter_context(tc.tile_pool(name="stage", bufs=STAGE_BUFS))
        early_pool = stack.enter_context(tc.tile_pool(name="early", bufs=EARLY_BUFS))
        mx_pool = stack.enter_context(tc.tile_pool(name="mx", bufs=MX_BUFS))
        tail_pool = stack.enter_context(tc.tile_pool(name="tail", bufs=2))
        bank_pool = stack.enter_context(tc.psum_pool(name="bank", bufs=4))
        acc_pool = stack.enter_context(tc.psum_pool(name="acc", bufs=1))

        ident = const.tile([P, P], F32)
        make_identity(nc, ident[:])

        def channels_to_partitions(words, words_per_channel, pair):
            bank = bank_pool.tile([P, PACK, P], F32, tag="bank")
            for t in range(PACK):
                first = words_per_channel * t + pair
                nc.tensor.transpose(
                    bank[:, t, :],
                    words[:, first : CHANNELS * words_per_channel : PACK * words_per_channel],
                    ident[:],
                )
            return bank

        def part_the_pair(on_vector, grouped, bank):
            halves = bank[:].bitcast(BF16).rearrange("p t (r e) -> p e r t", e=2)
            if on_vector:
                nc.vector.tensor_copy(out=grouped, in_=halves)
            else:
                nc.scalar.copy(out=grouped, in_=halves)

        b2_bf = const.tile([P, O_GROUPS * POSITIONS], BF16)
        b2_f32 = const.tile([P, O_GROUPS * POSITIONS], F32)

        h_rows = h_pool1.rearrange("(a n) c r s -> a n (c r s)", n=P)
        h_words = []
        for first in range(0, BATCH_TILES, 2):
            h_raw = raw_pool.tile([P, 2, CHANNELS * PIXELS], BF16, tag="raw")
            for a in (first, first + 1):
                nc.sync.dma_start(out=h_raw[:, a - first, :], in_=h_rows[a])
                h_words.append(h_raw[:, a - first, :].bitcast(F32))

        nc.sync.dma_start(out=b2_bf[:], in_=b2.rearrange("(m g) i j -> m (g i j)", g=O_GROUPS))

        w_rows = w2.rearrange("(m g) c k i j -> g m (c k i j)", g=O_GROUPS)
        w_quads = w2.rearrange("(m g) (p t) k i j -> g p m (t k i j)", g=O_GROUPS, t=PACK)
        w_raws = []
        for group in range(O_GROUPS):
            if group < W_GROUPS_BY_TRANSPOSE:
                w_raw = raw_pool.tile([P, CHANNELS * PLANES], BF16, tag="raw")
                piece = CHANNELS * PLANES // W_LOAD_PIECES
                for q in range(W_LOAD_PIECES):
                    cols = slice(q * piece, (q + 1) * piece)
                    nc.sync.dma_start(out=w_raw[:, cols], in_=w_rows[group][:, cols])
            else:
                w_raw = raw_pool.tile([P, P, PACK * PLANES], BF16, tag="raw")
                piece = P // W_LOAD_PIECES
                for q in range(W_LOAD_PIECES):
                    rows = slice(q * piece, (q + 1) * piece)
                    nc.sync.dma_start(out=w_raw[:, rows, :], in_=w_quads[group][:, rows, :])
            w_raws.append(w_raw)

        fc_words = const.tile([P, FEATURES * PACK], U8, align_bytes=64)
        fc_scales = const.tile([P, FEATURES], U8, align_bytes=64)
        nc.vector.memset(fc_scales[:].bitcast(I32), 0)
        nc.sync.dma_start(
            out=fc_words[:].bitcast(I32),
            in_=fc1_w_words.rearrange("g p n t -> (g p) (n t)").bitcast(I32),
        )
        scale_rows = fc1_w_scales.rearrange("g q n -> (g q) n").bitcast(I32)
        for quadrant in range(4):
            nc.sync.dma_start(
                out=fc_scales[32 * quadrant : 32 * quadrant + 4, :].bitcast(I32),
                in_=scale_rows[4 * quadrant : 4 * quadrant + 4, :],
            )
        fc_bias = const.tile([P, FEATURES], BF16)
        nc.sync.dma_start(out=fc_bias[:], in_=fc1_b.partition_broadcast(P))

        h_codes = const.tile([P, PIXELS, BATCH], U32, align_bytes=64)
        h_scales = const.tile([P, PIXELS, BATCH], U8, align_bytes=64)
        H_PAIRS = PIXELS // 2
        h_steps = [(a, pair) for a in range(BATCH_TILES) for pair in range(H_PAIRS)]
        h_grouped = {}
        for step in range(len(h_steps) + 1):
            if step < len(h_steps):
                a, pair = h_steps[step]
                bank = channels_to_partitions(h_words[a], H_PAIRS, pair)
                grouped = grouped_pool.tile([P, 2, P, PACK], BF16, tag="grouped", align_bytes=64)
                part_the_pair(step % H_V[1] in H_V[0], grouped[:], bank)
                h_grouped[step] = grouped
            if step >= 1:
                a, pair = h_steps[step - 1]
                images = slice(a * P, (a + 1) * P)
                for e in range(2):
                    nc.vector.quantize_mx(
                        out=h_codes[:, 2 * pair + e, images].bitcast(FP8X4),
                        scales=h_scales[:, 2 * pair + e, images],
                        in_=h_grouped[step - 1][:, e].rearrange("p r t -> p (r t)"),
                    )

        g_grouped = const.tile([P, BATCH, PACK], BF16, align_bytes=64)
        g_lines = const.tile([P, PACK, BATCH], BF16, align_bytes=64)
        nc.vector.tensor_copy(out=b2_f32[:], in_=b2_bf[:])
        W_PAIRS = PLANES // 2
        grouped_of = {}
        codes_of = {}
        scales_of = {}
        acc = {}
        sums_of = {}

        def fetch_by_transposes(unit, for_vector):
            group, k = divmod(unit, OFFSETS)
            grouped = grouped_pool.tile([P, POSITIONS, P, PACK], BF16, tag="grouped", align_bytes=64)
            for i in range(OUT_SIDE):
                bank = channels_to_partitions(w_raws[group][:].bitcast(F32), W_PAIRS, OUT_SIDE * k + i)
                part_the_pair(i in for_vector, grouped[:, OUT_SIDE * i : OUT_SIDE * (i + 1)], bank)
            grouped_of[unit] = grouped[:]

        stage_of = {}

        def reorder(unit, on_vector):
            group, k = divmod(unit, OFFSETS)
            stage = stage_pool.tile([P, POSITIONS, 2, P, 2], BF16, tag="stage", align_bytes=64, name="stage")
            planes = w_raws[group][:].rearrange("m (p u e k s) -> m k u p e s", p=P, u=2, e=2, k=OFFSETS)[:, k]
            spread = stage[:].rearrange("m s u p e -> m u p e s")
            if on_vector:
                nc.vector.tensor_copy(out=spread, in_=planes)
            else:
                nc.scalar.copy(out=spread, in_=planes)
            stage_of[unit] = stage

        def fetch_reordered(unit, for_vector):
            grouped = grouped_pool.tile([P, POSITIONS, P, PACK], BF16, tag="grouped", align_bytes=64)
            words = stage_of[unit][:].rearrange("m s u p e -> m (s u p e)").bitcast(F32)
            for i in range(OUT_SIDE):
                bank = bank_pool.tile([P, 2, 2, P], F32, tag="bank", name="bank")
                for s in range(2):
                    for u in range(2):
                        first = ((OUT_SIDE * i + s) * 2 + u) * P
                        nc.tensor.transpose(bank[:, s, u, :], words[:, first : first + P], ident[:])
                half = grouped[:, OUT_SIDE * i : OUT_SIDE * (i + 1)].rearrange("p s m t -> p (s m t)").bitcast(F32)
                out = half.rearrange("p (j m u) -> p j m u", j=2, u=2)
                in_ = bank[:].rearrange("p j u m -> p j m u")
                if i in for_vector:
                    nc.vector.tensor_copy(out=out, in_=in_)
                else:
                    nc.scalar.copy(out=out, in_=in_)
            grouped_of[unit] = grouped[:]

        def copy_rows(unit, first, last, on_vector):
            group, k = divmod(unit, OFFSETS)
            if unit not in grouped_of:
                early = unit - OFFSETS * 2 in {e[1] for e in EARLY}
                tile = (early_pool if early else grouped_pool).tile(
                    [P, POSITIONS, P, PACK], BF16, tag="grouped", align_bytes=64, name="grouped"
                )
                grouped_of[unit] = tile[:]
            rows = slice(first, last)
            planes = w_raws[group][:, rows, :].rearrange("p m (t k s) -> p k m t s", t=PACK, k=OFFSETS)[:, k]
            spread = grouped_of[unit][:, :, rows, :].rearrange("p s m t -> p m t s")
            if on_vector:
                nc.vector.tensor_copy(out=spread, in_=planes)
            else:
                nc.scalar.copy(out=spread, in_=planes)

        def quantise(unit):
            codes = mx_pool.tile([P, POSITIONS, P], U32, name="w_codes", align_bytes=64)
            scales = mx_pool.tile([P, POSITIONS, P], U8, name="w_scales", align_bytes=64)
            nc.vector.quantize_mx(
                out=codes[:].rearrange("p s m -> p (s m)").bitcast(FP8X4),
                scales=scales[:].rearrange("p s m -> p (s m)"),
                in_=grouped_of[unit].rearrange("p s m t -> p (s m t)"),
            )
            codes_of[unit] = codes
            scales_of[unit] = scales

        def pass_of(unit, pos):
            group, k = divmod(unit, OFFSETS)
            di, dj = divmod(k, KS)
            i, j = divmod(pos, OUT_SIDE)
            pixel = (i + di) * SIDE + (j + dj)
            if k == 0:
                if group % 2 == 1:
                    acc[pos] = bank_pool.tile([P, BATCH], F32, tag="bank", name="late_acc")
                else:
                    acc[pos] = acc_pool.tile([P, BATCH], F32, name="acc%d" % pos)
            nc.tensor.matmul_mx(
                out=acc[pos][:],
                lhsT=codes_of[unit][:, pos, :].bitcast(FP8X4),
                lhsT_scale=scales_of[unit][:, pos, :],
                rhs=h_codes[:, pixel, :].bitcast(FP8X4),
                rhs_scale=h_scales[:, pixel, :],
                start=(k == 0),
                stop=(k == OFFSETS - 1),
            )

        def multiply(unit):
            group, k = divmod(unit, OFFSETS)
            if unit >= UNITS - LATE:
                if unit == UNITS - 1:
                    for pos in range(POSITIONS):
                        for late in range(UNITS - LATE, UNITS):
                            pass_of(late, pos)
            else:
                for pos in range(POSITIONS):
                    pass_of(unit, pos)
            if k == OFFSETS - 1:
                sums_of[group] = dict(acc)
                if group < O_GROUPS - 1:
                    due.append((unit + POOL_LAG[group], group))

        def pool_first(group, images):
            best = tail_pool.tile([P, images.stop - images.start], F32, tag="best", name="best")
            nc.scalar.activation(
                out=best[:],
                in_=sums_of[group][0][:, images],
                func=RELU,
                bias=b2_f32[:, POSITIONS * group : POSITIONS * group + 1],
            )
            return best

        def pool_next(group, pos, images, best, out):
            col = POSITIONS * group + pos
            nc.vector.scalar_tensor_tensor(
                out=out,
                in0=sums_of[group][pos][:, images],
                scalar=b2_f32[:, col : col + 1],
                in1=best[:],
                op0=ADD,
                op1=MAX,
            )

        def pool_but_the_last(group):
            images = slice(0, BATCH)
            best = pool_first(group, images)
            for pos in (1, 2):
                better = tail_pool.tile([P, BATCH], F32, tag=("best", "relu_left")[pos % 2], name="better")
                pool_next(group, pos, images, best, better[:])
                best = better
            return best

        pool_steps = []

        def pooling(group):
            images = slice(0, BATCH)
            best = [pool_first(group, images)]

            def step(pos):
                if pos < POSITIONS - 1:
                    better = tail_pool.tile([P, BATCH], F32, tag=("best", "relu_left")[pos % 2], name="better")
                    pool_next(group, pos, images, best[0], better[:])
                    best[0] = better
                else:
                    pool_next(group, pos, images, best[0], g_lines[:, group, :])

            for pos in range(1, POSITIONS):
                pool_steps.append((step, pos))

        def pool_step():
            if pool_steps:
                step, pos = pool_steps.pop(0)
                step(pos)

        due = []
        to_multiply = list(range(UNITS))
        ready = set()

        def multiply_next():
            if to_multiply and to_multiply[0] in codes_of:
                unit = to_multiply.pop(0)
                multiply(unit)
                while due and due[0][0] <= unit:
                    pooling(due.pop(0)[1])

        rounds = [
            [OFFSETS * group + k for k in ks]
            for group in range(W_GROUPS_BY_TRANSPOSE)
            for ks in ROUNDS_OF_A_GROUP
        ]
        third = list(range(OFFSETS * 2, OFFSETS * 3))
        fourth = list(range(OFFSETS * 3, UNITS))
        for n, unit in enumerate(rounds[0]):
            if REORDER[n] and FIRST_RE == 0:
                reorder(unit, REORDER[n] == "V")
        waiting = []
        for r, units in enumerate(rounds):
            if r + 1 < len(rounds):
                for n, unit in enumerate(rounds[r + 1]):
                    if REORDER[n] and r + 1 >= FIRST_RE:
                        reorder(unit, REORDER[n] == "V")
            if QLATE:
                for unit in waiting:
                    quantise(unit)
            for rr, n, first, last, vec in EARLY:
                if rr == r:
                    copy_rows(third[n], first, last, vec)
            for n, unit in enumerate(units):
                if unit in stage_of:
                    fetch_reordered(unit, VEC_RE)
                else:
                    fetch_by_transposes(unit, VEC_BANKS[r % 2] if n == 0 else VEC_BANKS[2])
            if not QLATE:
                for unit in units:
                    quantise(unit)
            for n in range(MX_IN_ROUND[r]):
                if to_multiply[0] in ready:
                    multiply_next()
            ready.update(units if not QLATE else waiting)
            waiting = units
        if QLATE:
            for unit in waiting:
                quantise(unit)
        begun = sorted({e[1] for e in EARLY})
        for n in begun:
            copy_rows(third[n], max(e[3] for e in EARLY if e[1] == n), P, n in BEGUN_V)
        for n, unit in enumerate(third):
            if n + len(begun) < OFFSETS:
                if SPLIT > 0:
                    copy_rows(third[n + len(begun)], 0, SPLIT, True)
                copy_rows(third[n + len(begun)], SPLIT, P, False)
            quantise(unit)
            pool_step()
            for n in range(MX_D2[n]):
                multiply_next()
        last_group = raw_pool.tile([P, OFFSETS, POSITIONS, P, PACK], BF16, tag="raw")
        for n, unit in enumerate(fourth):
            grouped_of[unit] = last_group[:, n]
        count = 0
        for first, last in PRE:
            for n, unit in enumerate(fourth):
                copy_rows(unit, first, last, n % PRE_V[1] < PRE_V[0])
                if n % PRE_V[1] < PRE_V[0]:
                    pool_step()
                count += 1
                if count % MX_PRE == 0:
                    multiply_next()
        for n, unit in enumerate(fourth):
            if n == 0:
                while pool_steps:
                    pool_step()
            copy_rows(unit, PRE[-1][1], P, n in LAST_V)
            if n >= 1:
                quantise(fourth[n - 1])
                pool_step()
                multiply_next()
        quantise(fourth[-1])
        while to_multiply:
            multiply_next()
            pool_step()
        while pool_steps:
            pool_step()
        best = pool_but_the_last(O_GROUPS - 1)
        g_codes = const.tile([P, BATCH], U32, align_bytes=64)
        g_scales = const.tile([P, BATCH], U8, align_bytes=64)
        for images in HALVES:
            pool_next(O_GROUPS - 1, POSITIONS - 1, images, best[:, images], g_lines[:, O_GROUPS - 1, images])
        for n, images in enumerate(HALVES):
            four = g_lines[:, :, images].rearrange("p t n -> p n t")
            if n == 0:
                nc.scalar.copy(out=g_grouped[:, images, :], in_=four)
            else:
                nc.vector.tensor_copy(out=g_grouped[:, images, :], in_=four)
        for images in HALVES[::-1]:
            nc.vector.quantize_mx(
                out=g_codes[:, images].bitcast(FP8X4),
                scales=g_scales[:, images],
                in_=g_grouped[:, images, :].rearrange("p n t -> p (n t)"),
            )
        for n, a in enumerate((2, 3, 0, 1)):
            images = slice(a * P, (a + 1) * P)
            dense = acc_pool.tile([P, FEATURES], F32, name="acc%d" % a)
            nc.tensor.matmul_mx(
                out=dense[:],
                lhsT=g_codes[:, images].bitcast(FP8X4),
                lhsT_scale=g_scales[:, images],
                rhs=fc_words[:].bitcast(FP8X4),
                rhs_scale=fc_scales[:],
                start=True,
                stop=True,
            )
            result = tail_pool.tile([P, FEATURES], F32, tag=("best", "relu_left")[n % 2], name="result")
            for cols in HALVES if n == 3 else (slice(0, FEATURES),):
                nc.vector.tensor_tensor(out=result[:, cols], in0=dense[:, cols], in1=fc_bias[:, cols], op=ADD)
                nc.scalar.activation(out=result[:, cols], in_=result[:, cols], func=RELU)
                nc.sync.dma_start(out=out[images, cols], in_=result[:, cols])
